import numpy as np
import ml_dtypes


def mxq(x, axis, fmt="e4m3"):
    dtype, down = {"e4m3": (ml_dtypes.float8_e4m3fn, 7), "e5m2": (ml_dtypes.float8_e5m2, 14)}[fmt]
    v = np.moveaxis(np.asarray(x, np.float32).astype(ml_dtypes.bfloat16).astype(np.float64), axis, -1)
    blocks = v.reshape(v.shape[:-1] + (-1, 32))
    amax = np.abs(blocks).max(-1, keepdims=True)
    byte = np.maximum(np.where(amax > 0, np.frexp(amax)[1] - 1 + 127, 0) - down, 1)
    scale = np.exp2(byte - 127.0)
    codes = (blocks / scale).astype(np.float32).astype(dtype).astype(np.float64)
    return np.moveaxis((codes * scale).reshape(v.shape), -1, axis)


WIDE = False


def mx_kscale(k):
    if not WIDE:
        return np.ones(k)
    levels = np.array([10, -10, 5, -5, 0])
    if k % 512:
        return np.exp2(np.random.permutation(np.resize(levels, k // 32))).repeat(32)
    a = np.empty((k // 512, 16))
    for p in range(k // 512):
        a[p, :8] = np.random.permutation(np.resize(levels, 8))
        for g in range(8):
            far = levels[np.abs(levels - a[p, g]) >= 10]
            a[p, g + 8] = far[np.random.randint(len(far))]
    return np.exp2(a.ravel()).repeat(32)


BF16 = ml_dtypes.bfloat16


def bf(x):
    return np.asarray(x, np.float32).astype(BF16)


def f64(x):
    return np.asarray(x).astype(np.float64)


B, S, D_MODEL, N_H, D_H, D_CQ, D_CKV, D_HR = 4, 1024, 1024, 4, 128, 512, 512, 128
ROPE_BASE = 10000.0


def rope_cos_sin(seq_len, dim):
    inv_freq = 1.0 / (ROPE_BASE ** (np.arange(0, dim, 2) / dim))
    ang = np.arange(seq_len)[:, None] * inv_freq[None, :]
    return np.cos(ang), np.sin(ang)


def rope(t, cos, sin):
    shp = t.shape
    d2 = shp[-1] // 2
    tr = t.reshape(shp[:-1] + (d2, 2))
    x0, x1 = tr[..., 0], tr[..., 1]
    bshape = (1, shp[1]) + (1,) * (x0.ndim - 3) + (d2,)
    cs, sn = cos.reshape(bshape), sin.reshape(bshape)
    return np.stack([x0 * cs - x1 * sn, x0 * sn + x1 * cs], axis=-1).reshape(shp)


def setup_inputs():
    s, t = mx_kscale(D_MODEL), mx_kscale(D_CQ)
    return {"h": bf(np.random.standard_normal((B, S, D_MODEL)) * s),
            "w_cq": bf(np.random.standard_normal((D_MODEL, D_CQ)) / np.sqrt(D_MODEL) / s[:, None] * t),
            "w_q": bf(np.random.standard_normal((D_CQ, N_H * D_H)) / np.sqrt(D_CQ) / t[:, None]),
            "w_qr": bf(np.random.standard_normal((D_CQ, N_H * D_HR)) / np.sqrt(D_CQ) / t[:, None])}


def reference(h, w_cq, w_q, w_qr):
    cos, sin = rope_cos_sin(S, D_HR)
    c_q = mxq(f64(h), 2, "e4m3") @ mxq(f64(w_cq), 0, "e4m3")
    cq = mxq(c_q, 2, "e4m3")
    q_c = (cq @ mxq(f64(w_q), 0, "e4m3")).reshape(B, S, N_H, D_H).transpose(0, 2, 1, 3)
    q_r = rope((cq @ mxq(f64(w_qr), 0, "e4m3")).reshape(B, S, N_H, D_HR), cos, sin).transpose(0, 2, 1, 3)
    return np.concatenate([q_c, q_r], axis=-1)

@@ -1,0 +1,297 @@
+import math
+from contextlib import ExitStack
+
+import concourse.mybir as mybir
+from concourse.masks import make_identity
+
+F32 = mybir.dt.float32
+BF16 = mybir.dt.bfloat16
+I32 = mybir.dt.int32
+U32 = mybir.dt.uint32
+U8 = mybir.dt.uint8
+FP8X4 = mybir.dt.float8_e4m3fn_x4
+MULT = mybir.AluOpType.mult
+ADD = mybir.AluOpType.add
+SUBTRACT = mybir.AluOpType.subtract
+SIN = mybir.ActivationFunctionType.Sin
+
+P = 128
+PACK = 4
+B, S, D_MODEL, N_H, D_H, D_CQ = 4, 1024, 1024, 4, 128, 512
+D_OUT = N_H * D_H
+PASSES_1 = D_MODEL // (P * PACK)
+TILES = S // P
+PAIRS = D_H // 2
+HALF = 4
+STEP = 2
+ROPE_BASE = 10000.0
+ROUND_MAGIC = 1.5 * 2.0**23
+
+FLOPS = 2 * B * S * (D_MODEL * D_CQ + D_CQ * 2 * D_OUT)
+
+
+def rope_turn_fractions(nc, pool):
+    position_i = pool.tile([P, TILES], I32)
+    nc.gpsimd.iota(position_i[:], pattern=[[1, TILES]], base=0, channel_multiplier=TILES)
+    position = pool.tile([P, TILES], F32)
+    nc.vector.tensor_copy(out=position[:], in_=position_i[:])
+
+    ratio = ROPE_BASE ** (-1.0 / PAIRS)
+    freq = pool.tile([P, PAIRS], F32)
+    nc.vector.memset(freq[:, 0:1], 1.0)
+    for level in range(6):
+        w = 2**level
+        nc.vector.tensor_scalar_mul(out=freq[:, w : 2 * w], in0=freq[:, 0:w], scalar1=ratio**w)
+
+    shape = [P, TILES, PAIRS]
+    turns = pool.tile(shape, F32)
+    nc.vector.scalar_tensor_tensor(
+        out=turns[:],
+        in0=freq[:].unsqueeze(1).to_broadcast(shape),
+        scalar=1.0 / (2.0 * math.pi),
+        in1=position[:].unsqueeze(2).to_broadcast(shape),
+        op0=MULT,
+        op1=MULT,
+    )
+    quarter = pool.tile(shape, F32)
+    nc.vector.tensor_scalar_add(out=quarter[:], in0=turns[:], scalar1=0.25)
+
+    fractions = []
+    for name, angle in (("sin", turns), ("cos", quarter)):
+        whole = pool.tile(shape, F32, name="whole_" + name)
+        nc.vector.tensor_scalar(
+            out=whole[:], in0=angle[:], scalar1=ROUND_MAGIC, scalar2=ROUND_MAGIC, op0=ADD, op1=SUBTRACT
+        )
+        fraction = pool.tile(shape, F32, name="fraction_" + name)
+        nc.vector.tensor_sub(out=fraction[:], in0=angle[:], in1=whole[:])
+        fractions.append(fraction)
+    return fractions
+
+
+def rope_table(nc, pool, sin_fraction, cos_fraction):
+    table = pool.tile([P, TILES, 3, PAIRS], F32)
+    nc.scalar.activation(out=table[:, :, 0, :], in_=sin_fraction[:], func=SIN, scale=-2.0 * math.pi)
+    nc.scalar.activation(out=table[:, :, 2, :], in_=sin_fraction[:], func=SIN, scale=2.0 * math.pi)
+    nc.scalar.activation(out=table[:, :, 1, :], in_=cos_fraction[:], func=SIN, scale=2.0 * math.pi)
+    return table
+
+
+def regroup(copy, grouped, raw):
+    copy(
+        out=grouped.rearrange("p (c i) t -> p c t i", i=4),
+        in_=raw.rearrange("p t (c i) -> p c t i", i=4),
+    )
+
+
+def tile_mla_pa_t_kernel(tc, h, w_cq, w_q, w_qr, out):
+    nc = tc.nc
+    with ExitStack() as ctx:
+        ctx.enter_context(tc.manual_schedule())
+        consts = ctx.enter_context(tc.tile_pool(name="consts", bufs=1))
+        x_pool = ctx.enter_context(tc.tile_pool(name="x", bufs=B * TILES // HALF))
+        work = ctx.enter_context(tc.tile_pool(name="work", bufs=3))
+        out_pool = ctx.enter_context(tc.tile_pool(name="outs", bufs=3))
+        psum = ctx.enter_context(tc.psum_pool(name="psum", bufs=STEP))
+
+        halves = [(b, half) for b in range(B) for half in range(TILES // HALF)]
+        x_tiles = {}
+        for b, half in halves:
+            x_tiles[(b, half)] = x_pool.tile([P, HALF, D_MODEL], BF16, name="x")
+
+        def load_h(b, half, first, count):
+            rows = h[b].rearrange("(p t) k -> p t k", t=TILES)
+            nc.sync.dma_start(
+                out=x_tiles[(b, half)][:, first : first + count, :],
+                in_=rows[:, half * HALF + first : half * HALF + first + count, :],
+            )
+
+        wc_raw = consts.tile([P, PASSES_1, PACK, D_CQ], BF16)
+        w2_raw = consts.tile([P, 2, PACK, D_OUT], BF16)
+        nc.sync.dma_start(
+            out=wc_raw[:].rearrange("p g j c -> p g (j c)"),
+            in_=w_cq.rearrange("(g p j) c -> p g (j c)", g=PASSES_1, j=PACK),
+        )
+        load_h(0, 0, 0, STEP)
+        load_h(0, 0, STEP, STEP)
+        nc.sync.dma_start(out=w2_raw[:, 0], in_=w_q.rearrange("(p j) n -> p j n", j=PACK))
+        nc.sync.dma_start(out=w2_raw[:, 1], in_=w_qr.rearrange("(p j) n -> p j n", j=PACK))
+        for b, half in halves[1:]:
+            load_h(b, half, 0, HALF)
+
+        sin_fraction, cos_fraction = rope_turn_fractions(nc, consts)
+        table = rope_table(nc, consts, sin_fraction, cos_fraction)
+        identity = consts.tile([P, P], F32)
+        make_identity(nc, identity[:])
+
+        wc_grouped = consts.tile([P, PASSES_1, D_CQ, PACK], BF16, align_bytes=64)
+        wc_codes = consts.tile([P, PASSES_1, D_CQ], U32, align_bytes=64)
+        wc_scales = consts.tile([P, PASSES_1, D_CQ], U8, align_bytes=64)
+        for g in range(PASSES_1):
+            nc.vector.tensor_copy(
+                out=wc_grouped[:, g].rearrange("p (t m) j -> p m t j", t=PACK),
+                in_=wc_raw[:, g].rearrange("p j (m t) -> p m t j", t=PACK),
+            )
+        nc.vector.quantize_mx(
+            out=wc_codes[:].rearrange("p g c -> p (g c)").bitcast(FP8X4),
+            scales=wc_scales[:].rearrange("p g c -> p (g c)"),
+            in_=wc_grouped[:].rearrange("p g c t -> p (g c t)"),
+        )
+        w2_grouped = consts.tile([P, 2, D_OUT, PACK], BF16, align_bytes=64)
+        w2_codes = consts.tile([P, 2, D_OUT], U32, align_bytes=64)
+        w2_scales = consts.tile([P, 2, D_OUT], U8, align_bytes=64)
+
+        def quantise_second_weights():
+            regroup(nc.vector.tensor_copy, w2_grouped[:, 0], w2_raw[:, 0])
+            regroup(nc.scalar.copy, w2_grouped[:, 1], w2_raw[:, 1])
+            nc.vector.quantize_mx(
+                out=w2_codes[:].rearrange("p w c -> p (w c)").bitcast(FP8X4),
+                scales=w2_scales[:].rearrange("p w c -> p (w c)"),
+                in_=w2_grouped[:].rearrange("p w c t -> p (w c t)"),
+            )
+
+        steps = [(b, first) for b in range(B) for first in range(0, TILES, STEP)]
+        h_grouped = {}
+        h_mx = {}
+        c_grouped = {}
+        c_mx = {}
+        out_tiles = {}
+        u_banks = {}
+
+        def transpose_h(n):
+            b, first = steps[n]
+            x_words = x_tiles[(b, first // HALF)][:].rearrange("p t k -> p (t k)").bitcast(F32)
+            h_grouped[n] = work.tile([P, STEP * PASSES_1 * P * PACK], BF16, name="h_grouped", align_bytes=64)
+            grouped_words = h_grouped[n][:].bitcast(F32).rearrange(
+                "p (i g r u) -> p i g r u", i=STEP, g=PASSES_1, u=2
+            )
+            banks = []
+            for i in range(STEP):
+                xt = psum.tile([P, 2 * PASSES_1, P], F32, name="xt")
+                for g in range(PASSES_1):
+                    word0 = ((first + i) % HALF) * (D_MODEL // 2) + g * 2 * P
+                    for u in range(2):
+                        nc.tensor.transpose(
+                            xt[:, 2 * g + u, :], x_words[:, word0 + u : word0 + 2 * P : 2], identity[:]
+                        )
+                banks.append(xt)
+            for i in range(STEP):
+                nc.scalar.copy(out=grouped_words[:, i], in_=banks[i][:].rearrange("p (g u) r -> p g r u", u=2))
+
+        def quantise_h(n):
+            codes = work.tile([P, STEP, PASSES_1, P], U32, name="h_codes", align_bytes=64)
+            scales = work.tile([P, STEP, PASSES_1, P], U8, name="h_scales", align_bytes=64)
+            nc.vector.quantize_mx(
+                out=codes[:].rearrange("p i g r -> p (i g r)").bitcast(FP8X4),
+                scales=scales[:].rearrange("p i g r -> p (i g r)"),
+                in_=h_grouped[n][:],
+            )
+            h_mx[n] = (codes, scales)
+
+        def compress(n):
+            codes_h, scales_h = h_mx[n]
+            c_grouped[n] = work.tile([P, STEP, P, PACK], BF16, name="c_grouped", align_bytes=64)
+            banks = []
+            for i in range(STEP):
+                cq = psum.tile([P, PACK, P], F32, name="cq")
+                for t in range(PACK):
+                    for g in range(PASSES_1):
+                        nc.tensor.matmul_mx(
+                            out=cq[:, t, :],
+                            lhsT=wc_codes[:, g, t * P : (t + 1) * P].bitcast(FP8X4),
+                            lhsT_scale=wc_scales[:, g, t * P : (t + 1) * P],
+                            rhs=codes_h[:, i, g, :].bitcast(FP8X4),
+                            rhs_scale=scales_h[:, i, g, :],
+                            start=(g == 0),
+                            stop=(g == PASSES_1 - 1),
+                        )
+                banks.append(cq)
+            for i in range(STEP):
+                nc.scalar.copy(out=c_grouped[n][:, i], in_=banks[i][:].rearrange("p t r -> p r t"))
+
+        def quantise_c(n):
+            codes = work.tile([P, STEP, P], U32, name="c_codes", align_bytes=64)
+            scales = work.tile([P, STEP, P], U8, name="c_scales", align_bytes=64)
+            nc.vector.quantize_mx(
+                out=codes[:].rearrange("p i r -> p (i r)").bitcast(FP8X4),
+                scales=scales[:].rearrange("p i r -> p (i r)"),
+                in_=c_grouped[n][:].rearrange("p i r t -> p (i r t)"),
+            )
+            c_mx[n] = (codes, scales)
+
+        def store(b, first, count):
+            rows = out[b].rearrange("n (p t) f -> p n t f", t=TILES)
+            q_tile = out_tiles[(b, first // HALF)]
+            nc.sync.dma_start(
+                out=rows[:, :, first : first + count, :],
+                in_=q_tile[:, :, first % HALF : first % HALF + count, :],
+            )
+
+        def project(n):
+            b, first = steps[n]
+            codes_c, scales_c = c_mx[n]
+            if first % HALF == 0:
+                out_tiles[(b, first // HALF)] = out_pool.tile([P, N_H, HALF, 2 * D_H], F32, name="q_tile")
+            q_tile = out_tiles[(b, first // HALF)]
+            banks = []
+            for i in range(STEP):
+                for which, name in enumerate(("a_ps", "u_ps")):
+                    product = psum.tile([P, D_OUT], F32, name=name)
+                    nc.tensor.matmul_mx(
+                        out=product[:],
+                        lhsT=codes_c[:, i, :].bitcast(FP8X4),
+                        lhsT_scale=scales_c[:, i, :],
+                        rhs=w2_codes[:, which, :].bitcast(FP8X4),
+                        rhs_scale=w2_scales[:, which, :],
+                        start=True,
+                        stop=True,
+                    )
+                    banks.append(product)
+            for i in range(STEP):
+                t = first + i
+                nc.scalar.copy(
+                    out=q_tile[:, :, t % HALF, 0:D_H], in_=banks[2 * i][:].rearrange("p (n f) -> p n f", n=N_H)
+                )
+                u_banks[(n, i)] = banks[2 * i + 1]
+
+        def rotate(n, i):
+            b, first = steps[n]
+            q_tile = out_tiles[(b, first // HALF)]
+            products = work.tile([P, 2, N_H, PAIRS, 2], F32, name="products")
+            u_pairs = u_banks[(n, i)][:].rearrange("p (n i x) -> p n i x", n=N_H, x=2)
+            for x in range(2):
+                factors = table[:, first + i, 1 - x : 3 - x, :].rearrange("p e i -> p i e")
+                nc.vector.tensor_tensor(
+                    out=products[:, x],
+                    in0=u_pairs[:, :, :, x].unsqueeze(3).to_broadcast([P, N_H, PAIRS, 2]),
+                    in1=factors.unsqueeze(1).to_broadcast([P, N_H, PAIRS, 2]),
+                    op=MULT,
+                )
+            nc.gpsimd.tensor_tensor(
+                out=q_tile[:, :, (first + i) % HALF, D_H : 2 * D_H],
+                in0=products[:, 0].rearrange("p n i e -> p n (i e)"),
+                in1=products[:, 1].rearrange("p n i e -> p n (i e)"),
+                op=ADD,
+            )
+            if n >= len(steps) - HALF // STEP:
+                store(b, first + i, 1)
+            elif (first + i + 1) % HALF == 0:
+                store(b, first + i + 1 - HALF, HALF)
+
+        transpose_h(0)
+        quantise_h(0)
+        transpose_h(1)
+        quantise_h(1)
+        quantise_second_weights()
+        compress(0)
+        quantise_c(0)
+        for n in range(2, len(steps) + 2):
+            if n < len(steps):
+                transpose_h(n)
+                quantise_h(n)
+            if n <= len(steps):
+                compress(n - 1)
+            project(n - 2)
+            rotate(n - 2, 0)
+            if n <= len(steps):
+                quantise_c(n - 1)
+            rotate(n - 2, 1)

@@ -14,6 +14,7 @@ MULT = mybir.AluOpType.mult
 ADD = mybir.AluOpType.add
 SUBTRACT = mybir.AluOpType.subtract
 SIN = mybir.ActivationFunctionType.Sin
+ABS = mybir.ActivationFunctionType.Abs
 
 P = 128
 PACK = 4
@@ -30,18 +31,27 @@ ROUND_MAGIC = 1.5 * 2.0**23
 FLOPS = 2 * B * S * (D_MODEL * D_CQ + D_CQ * 2 * D_OUT)
 
 
-def rope_turn_fractions(nc, pool):
-    position_i = pool.tile([P, TILES], I32)
-    nc.gpsimd.iota(position_i[:], pattern=[[1, TILES]], base=0, channel_multiplier=TILES)
+def rope_turns(nc, pool):
     position = pool.tile([P, TILES], F32)
-    nc.vector.tensor_copy(out=position[:], in_=position_i[:])
-
+    nc.gpsimd.iota(
+        position[:],
+        pattern=[[1, TILES]],
+        base=0,
+        channel_multiplier=TILES,
+        allow_small_or_imprecise_dtypes=True,
+    )
     ratio = ROPE_BASE ** (-1.0 / PAIRS)
     freq = pool.tile([P, PAIRS], F32)
     nc.vector.memset(freq[:, 0:1], 1.0)
-    for level in range(6):
-        w = 2**level
-        nc.vector.tensor_scalar_mul(out=freq[:, w : 2 * w], in0=freq[:, 0:w], scalar1=ratio**w)
+    quarter_turn = pool.tile([P, 1], F32)
+    nc.vector.tensor_scalar(
+        out=quarter_turn[:], in0=freq[:, 0:1], scalar1=math.pi / 2.0, scalar2=0.0, op0=MULT, op1=ADD
+    )
+    for w in (1, 4, 16):
+        for k in range(1, 4):
+            nc.vector.tensor_scalar_mul(
+                out=freq[:, k * w : (k + 1) * w], in0=freq[:, 0:w], scalar1=ratio ** (k * w)
+            )
 
     shape = [P, TILES, PAIRS]
     turns = pool.tile(shape, F32)
@@ -53,27 +63,29 @@ def rope_turn_fractions(nc, pool):
         op0=MULT,
         op1=MULT,
     )
-    quarter = pool.tile(shape, F32)
-    nc.vector.tensor_scalar_add(out=quarter[:], in0=turns[:], scalar1=0.25)
-
-    fractions = []
-    for name, angle in (("sin", turns), ("cos", quarter)):
-        whole = pool.tile(shape, F32, name="whole_" + name)
-        nc.vector.tensor_scalar(
-            out=whole[:], in0=angle[:], scalar1=ROUND_MAGIC, scalar2=ROUND_MAGIC, op0=ADD, op1=SUBTRACT
-        )
-        fraction = pool.tile(shape, F32, name="fraction_" + name)
-        nc.vector.tensor_sub(out=fraction[:], in0=angle[:], in1=whole[:])
-        fractions.append(fraction)
-    return fractions
+    return turns, quarter_turn
 
 
-def rope_table(nc, pool, sin_fraction, cos_fraction):
-    table = pool.tile([P, TILES, 3, PAIRS], F32)
-    nc.scalar.activation(out=table[:, :, 0, :], in_=sin_fraction[:], func=SIN, scale=-2.0 * math.pi)
-    nc.scalar.activation(out=table[:, :, 2, :], in_=sin_fraction[:], func=SIN, scale=2.0 * math.pi)
-    nc.scalar.activation(out=table[:, :, 1, :], in_=cos_fraction[:], func=SIN, scale=2.0 * math.pi)
-    return table
+def turn_fractions(nc, pool, turns):
+    shape = [P, TILES, PAIRS]
+    whole = pool.tile(shape, F32)
+    nc.vector.tensor_scalar(
+        out=whole[:], in0=turns[:], scalar1=ROUND_MAGIC, scalar2=ROUND_MAGIC, op0=ADD, op1=SUBTRACT
+    )
+    fraction = pool.tile(shape, F32)
+    nc.vector.tensor_sub(out=fraction[:], in0=turns[:], in1=whole[:])
+    return fraction
+
+
+def fill_rope_table(nc, table, size, fraction, quarter_turn, t0, t1):
+    turn = 2.0 * math.pi
+    part = fraction[:, t0:t1]
+    nc.scalar.activation(out=table[:, t0:t1, 2, :], in_=part, func=SIN, scale=turn)
+    nc.scalar.activation(out=size[:, t0:t1], in_=part, func=ABS)
+    nc.scalar.activation(out=table[:, t0:t1, 0, :], in_=part, func=SIN, scale=-turn)
+    nc.scalar.activation(
+        out=table[:, t0:t1, 1, :], in_=size[:, t0:t1], func=SIN, scale=-turn, bias=quarter_turn[:]
+    )
 
 
 def regroup(copy, grouped, raw):
@@ -107,10 +119,10 @@ def tile_mla_pa_t_kernel(tc, h, w_cq, w_q, w_qr, out):
 
         wc_raw = consts.tile([P, PASSES_1, PACK, D_CQ], BF16)
         w2_raw = consts.tile([P, 2, PACK, D_OUT], BF16)
-        nc.sync.dma_start(
-            out=wc_raw[:].rearrange("p g j c -> p g (j c)"),
-            in_=w_cq.rearrange("(g p j) c -> p g (j c)", g=PASSES_1, j=PACK),
-        )
+        for g in range(PASSES_1):
+            nc.sync.dma_start(
+                out=wc_raw[:, g], in_=w_cq.rearrange("(g p j) c -> g p j c", g=PASSES_1, j=PACK)[g]
+            )
         load_h(0, 0, 0, STEP)
         load_h(0, 0, STEP, STEP)
         nc.sync.dma_start(out=w2_raw[:, 0], in_=w_q.rearrange("(p j) n -> p j n", j=PACK))
@@ -118,35 +130,28 @@ def tile_mla_pa_t_kernel(tc, h, w_cq, w_q, w_qr, out):
         for b, half in halves[1:]:
             load_h(b, half, 0, HALF)
 
-        sin_fraction, cos_fraction = rope_turn_fractions(nc, consts)
-        table = rope_table(nc, consts, sin_fraction, cos_fraction)
         identity = consts.tile([P, P], F32)
         make_identity(nc, identity[:])
+        turns, quarter_turn = rope_turns(nc, consts)
 
         wc_grouped = consts.tile([P, PASSES_1, D_CQ, PACK], BF16, align_bytes=64)
         wc_codes = consts.tile([P, PASSES_1, D_CQ], U32, align_bytes=64)
         wc_scales = consts.tile([P, PASSES_1, D_CQ], U8, align_bytes=64)
-        for g in range(PASSES_1):
-            nc.vector.tensor_copy(
-                out=wc_grouped[:, g].rearrange("p (t m) j -> p m t j", t=PACK),
-                in_=wc_raw[:, g].rearrange("p j (m t) -> p m t j", t=PACK),
-            )
-        nc.vector.quantize_mx(
-            out=wc_codes[:].rearrange("p g c -> p (g c)").bitcast(FP8X4),
-            scales=wc_scales[:].rearrange("p g c -> p (g c)"),
-            in_=wc_grouped[:].rearrange("p g c t -> p (g c t)"),
-        )
         w2_grouped = consts.tile([P, 2, D_OUT, PACK], BF16, align_bytes=64)
         w2_codes = consts.tile([P, 2, D_OUT], U32, align_bytes=64)
         w2_scales = consts.tile([P, 2, D_OUT], U8, align_bytes=64)
 
-        def quantise_second_weights():
-            regroup(nc.vector.tensor_copy, w2_grouped[:, 0], w2_raw[:, 0])
-            regroup(nc.scalar.copy, w2_grouped[:, 1], w2_raw[:, 1])
+        def regroup_first_weights(copy, g, m0, m1):
+            copy(
+                out=wc_grouped[:, g].rearrange("p (t m) j -> p m t j", t=PACK)[:, m0:m1],
+                in_=wc_raw[:, g].rearrange("p j (m t) -> p m t j", t=PACK)[:, m0:m1],
+            )
+
+        def quantise_weights(codes, scales, grouped, g):
             nc.vector.quantize_mx(
-                out=w2_codes[:].rearrange("p w c -> p (w c)").bitcast(FP8X4),
-                scales=w2_scales[:].rearrange("p w c -> p (w c)"),
-                in_=w2_grouped[:].rearrange("p w c t -> p (w c t)"),
+                out=codes[:, g].bitcast(FP8X4),
+                scales=scales[:, g],
+                in_=grouped[:, g].rearrange("p c j -> p (c j)"),
             )
 
         steps = [(b, first) for b in range(B) for first in range(0, TILES, STEP)]
@@ -218,12 +223,12 @@ def tile_mla_pa_t_kernel(tc, h, w_cq, w_q, w_qr, out):
             )
             c_mx[n] = (codes, scales)
 
-        def store(b, first, count):
+        def store(b, first, count, heads=slice(0, N_H)):
             rows = out[b].rearrange("n (p t) f -> p n t f", t=TILES)
             q_tile = out_tiles[(b, first // HALF)]
             nc.sync.dma_start(
-                out=rows[:, :, first : first + count, :],
-                in_=q_tile[:, :, first % HALF : first % HALF + count, :],
+                out=rows[:, heads, first : first + count, :],
+                in_=q_tile[:, heads, first % HALF : first % HALF + count, :],
             )
 
         def project(n):
@@ -256,35 +261,63 @@ def tile_mla_pa_t_kernel(tc, h, w_cq, w_q, w_qr, out):
         def rotate(n, i):
             b, first = steps[n]
             q_tile = out_tiles[(b, first // HALF)]
+            is_last = n == len(steps) - 1 and i == STEP - 1
             products = work.tile([P, 2, N_H, PAIRS, 2], F32, name="products")
             u_pairs = u_banks[(n, i)][:].rearrange("p (n i x) -> p n i x", n=N_H, x=2)
-            for x in range(2):
-                factors = table[:, first + i, 1 - x : 3 - x, :].rearrange("p e i -> p i e")
-                nc.vector.tensor_tensor(
-                    out=products[:, x],
-                    in0=u_pairs[:, :, :, x].unsqueeze(3).to_broadcast([P, N_H, PAIRS, 2]),
-                    in1=factors.unsqueeze(1).to_broadcast([P, N_H, PAIRS, 2]),
-                    op=MULT,
+            for n0, n1 in ((0, 2), (2, N_H)) if is_last else ((0, N_H),):
+                shape = [P, n1 - n0, PAIRS, 2]
+                for x in range(2):
+                    factors = table[:, first + i, 1 - x : 3 - x, :].rearrange("p e i -> p i e")
+                    nc.vector.tensor_tensor(
+                        out=products[:, x, n0:n1],
+                        in0=u_pairs[:, n0:n1, :, x].unsqueeze(3).to_broadcast(shape),
+                        in1=factors.unsqueeze(1).to_broadcast(shape),
+                        op=MULT,
+                    )
+                add = nc.vector.tensor_tensor if is_last else nc.gpsimd.tensor_tensor
+                add(
+                    out=q_tile[:, n0:n1, (first + i) % HALF, D_H : 2 * D_H],
+                    in0=products[:, 0, n0:n1].rearrange("p n i e -> p n (i e)"),
+                    in1=products[:, 1, n0:n1].rearrange("p n i e -> p n (i e)"),
+                    op=ADD,
                 )
-            nc.gpsimd.tensor_tensor(
-                out=q_tile[:, :, (first + i) % HALF, D_H : 2 * D_H],
-                in0=products[:, 0].rearrange("p n i e -> p n (i e)"),
-                in1=products[:, 1].rearrange("p n i e -> p n (i e)"),
-                op=ADD,
-            )
+                if is_last:
+                    store(b, first + i, 1, slice(n0, n1))
+            if is_last:
+                return
             if n >= len(steps) - HALF // STEP:
                 store(b, first + i, 1)
             elif (first + i + 1) % HALF == 0:
                 store(b, first + i + 1 - HALF, HALF)
 
+        fraction = turn_fractions(nc, consts, turns)
+        table = consts.tile([P, TILES, 3, PAIRS], F32)
+        size = consts.tile([P, TILES, PAIRS], F32)
+        fill_rope_table(nc, table, size, fraction, quarter_turn, 0, HALF)
+        regroup_first_weights(nc.vector.tensor_copy, 0, 0, P)
+        regroup_first_weights(nc.scalar.copy, 1, 0, P // 2)
+        regroup_first_weights(nc.vector.tensor_copy, 1, P // 2, P)
+        quantise_weights(wc_codes, wc_scales, wc_grouped, 0)
+        quantise_weights(wc_codes, wc_scales, wc_grouped, 1)
         transpose_h(0)
         quantise_h(0)
         transpose_h(1)
-        quantise_h(1)
-        quantise_second_weights()
         compress(0)
+        regroup(nc.vector.tensor_copy, w2_grouped[:, 0], w2_raw[:, 0])
+        quantise_h(1)
+        quantise_weights(w2_codes, w2_scales, w2_grouped, 0)
         quantise_c(0)
-        for n in range(2, len(steps) + 2):
+        regroup(nc.vector.tensor_copy, w2_grouped[:, 1], w2_raw[:, 1])
+        transpose_h(2)
+        compress(1)
+        quantise_weights(w2_codes, w2_scales, w2_grouped, 1)
+        project(0)
+        quantise_h(2)
+        rotate(0, 0)
+        quantise_c(1)
+        rotate(0, 1)
+        fill_rope_table(nc, table, size, fraction, quarter_turn, HALF, TILES)
+        for n in range(3, len(steps) + 2):
             if n < len(steps):
                 transpose_h(n)
                 quantise_h(n)

@@ -179,7 +179,7 @@ def tile_mla_pa_t_kernel(tc, h, w_cq, w_q, w_qr, out):
                             xt[:, 2 * g + u, :], x_words[:, word0 + u : word0 + 2 * P : 2], identity[:]
                         )
                 banks.append(xt)
-            for i in range(STEP):
+            for i in reversed(range(STEP)):
                 nc.scalar.copy(out=grouped_words[:, i], in_=banks[i][:].rearrange("p (g u) r -> p g r u", u=2))
 
         def quantise_h(n):
@@ -210,7 +210,7 @@ def tile_mla_pa_t_kernel(tc, h, w_cq, w_q, w_qr, out):
                             stop=(g == PASSES_1 - 1),
                         )
                 banks.append(cq)
-            for i in range(STEP):
+            for i in reversed(range(STEP)):
                 nc.scalar.copy(out=c_grouped[n][:, i], in_=banks[i][:].rearrange("p t r -> p r t"))
 
         def quantise_c(n):
@@ -251,7 +251,7 @@ def tile_mla_pa_t_kernel(tc, h, w_cq, w_q, w_qr, out):
                         stop=True,
                     )
                     banks.append(product)
-            for i in range(STEP):
+            for i in reversed(range(STEP)):
                 t = first + i
                 nc.scalar.copy(
                     out=q_tile[:, :, t % HALF, 0:D_H], in_=banks[2 * i][:].rearrange("p (n f) -> p n f", n=N_H)

@@ -25,6 +25,7 @@ TILES = S // P
 PAIRS = D_H // 2
 HALF = 4
 STEP = 2
+STEADY = 3
 ROPE_BASE = 10000.0
 ROUND_MAGIC = 1.5 * 2.0**23
 
@@ -77,15 +78,12 @@ def turn_fractions(nc, pool, turns):
     return fraction
 
 
-def fill_rope_table(nc, table, size, fraction, quarter_turn, t0, t1):
+def fill_rope_table(nc, table, size, fraction, quarter_turn):
     turn = 2.0 * math.pi
-    part = fraction[:, t0:t1]
-    nc.scalar.activation(out=table[:, t0:t1, 2, :], in_=part, func=SIN, scale=turn)
-    nc.scalar.activation(out=size[:, t0:t1], in_=part, func=ABS)
-    nc.scalar.activation(out=table[:, t0:t1, 0, :], in_=part, func=SIN, scale=-turn)
-    nc.scalar.activation(
-        out=table[:, t0:t1, 1, :], in_=size[:, t0:t1], func=SIN, scale=-turn, bias=quarter_turn[:]
-    )
+    nc.scalar.activation(out=table[:, :, 2, :], in_=fraction[:], func=SIN, scale=turn)
+    nc.scalar.activation(out=size[:], in_=fraction[:], func=ABS)
+    nc.scalar.activation(out=table[:, :, 0, :], in_=fraction[:], func=SIN, scale=-turn)
+    nc.scalar.activation(out=table[:, :, 1, :], in_=size[:], func=SIN, scale=-turn, bias=quarter_turn[:])
 
 
 def regroup(copy, grouped, raw):
@@ -126,8 +124,10 @@ def tile_mla_pa_t_kernel(tc, h, w_cq, w_q, w_qr, out):
         load_h(0, 0, 0, STEP)
         load_h(0, 0, STEP, STEP)
         nc.sync.dma_start(out=w2_raw[:, 0], in_=w_q.rearrange("(p j) n -> p j n", j=PACK))
+        load_h(0, 1, 0, STEP)
         nc.sync.dma_start(out=w2_raw[:, 1], in_=w_qr.rearrange("(p j) n -> p j n", j=PACK))
-        for b, half in halves[1:]:
+        load_h(0, 1, STEP, STEP)
+        for b, half in halves[2:]:
             load_h(b, half, 0, HALF)
 
         identity = consts.tile([P, P], F32)
@@ -141,10 +141,10 @@ def tile_mla_pa_t_kernel(tc, h, w_cq, w_q, w_qr, out):
         w2_codes = consts.tile([P, 2, D_OUT], U32, align_bytes=64)
         w2_scales = consts.tile([P, 2, D_OUT], U8, align_bytes=64)
 
-        def regroup_first_weights(copy, g, m0, m1):
-            copy(
-                out=wc_grouped[:, g].rearrange("p (t m) j -> p m t j", t=PACK)[:, m0:m1],
-                in_=wc_raw[:, g].rearrange("p j (m t) -> p m t j", t=PACK)[:, m0:m1],
+        def regroup_first_weights(g):
+            nc.vector.tensor_copy(
+                out=wc_grouped[:, g].rearrange("p (t m) j -> p m t j", t=PACK),
+                in_=wc_raw[:, g].rearrange("p j (m t) -> p m t j", t=PACK),
             )
 
         def quantise_weights(codes, scales, grouped, g):
@@ -161,6 +161,9 @@ def tile_mla_pa_t_kernel(tc, h, w_cq, w_q, w_qr, out):
         c_mx = {}
         out_tiles = {}
         u_banks = {}
+
+        def copy_order(n):
+            return range(STEP) if n < STEADY else range(STEP - 1, -1, -1)
 
         def transpose_h(n):
             b, first = steps[n]
@@ -179,7 +182,7 @@ def tile_mla_pa_t_kernel(tc, h, w_cq, w_q, w_qr, out):
                             xt[:, 2 * g + u, :], x_words[:, word0 + u : word0 + 2 * P : 2], identity[:]
                         )
                 banks.append(xt)
-            for i in reversed(range(STEP)):
+            for i in copy_order(n):
                 nc.scalar.copy(out=grouped_words[:, i], in_=banks[i][:].rearrange("p (g u) r -> p g r u", u=2))
 
         def quantise_h(n):
@@ -210,7 +213,7 @@ def tile_mla_pa_t_kernel(tc, h, w_cq, w_q, w_qr, out):
                             stop=(g == PASSES_1 - 1),
                         )
                 banks.append(cq)
-            for i in reversed(range(STEP)):
+            for i in copy_order(n):
                 nc.scalar.copy(out=c_grouped[n][:, i], in_=banks[i][:].rearrange("p t r -> p r t"))
 
         def quantise_c(n):
@@ -251,7 +254,7 @@ def tile_mla_pa_t_kernel(tc, h, w_cq, w_q, w_qr, out):
                         stop=True,
                     )
                     banks.append(product)
-            for i in reversed(range(STEP)):
+            for i in copy_order(n):
                 t = first + i
                 nc.scalar.copy(
                     out=q_tile[:, :, t % HALF, 0:D_H], in_=banks[2 * i][:].rearrange("p (n f) -> p n f", n=N_H)
@@ -285,18 +288,17 @@ def tile_mla_pa_t_kernel(tc, h, w_cq, w_q, w_qr, out):
                     store(b, first + i, 1, slice(n0, n1))
             if is_last:
                 return
-            if n >= len(steps) - HALF // STEP:
+            if n >= len(steps) - 2:
                 store(b, first + i, 1)
-            elif (first + i + 1) % HALF == 0:
-                store(b, first + i + 1 - HALF, HALF)
+            elif i == STEP - 1:
+                store(b, first, STEP)
 
         fraction = turn_fractions(nc, consts, turns)
         table = consts.tile([P, TILES, 3, PAIRS], F32)
         size = consts.tile([P, TILES, PAIRS], F32)
-        fill_rope_table(nc, table, size, fraction, quarter_turn, 0, HALF)
-        regroup_first_weights(nc.vector.tensor_copy, 0, 0, P)
-        regroup_first_weights(nc.scalar.copy, 1, 0, P // 2)
-        regroup_first_weights(nc.vector.tensor_copy, 1, P // 2, P)
+        fill_rope_table(nc, table, size, fraction, quarter_turn)
+        regroup_first_weights(0)
+        regroup_first_weights(1)
         quantise_weights(wc_codes, wc_scales, wc_grouped, 0)
         quantise_weights(wc_codes, wc_scales, wc_grouped, 1)
         transpose_h(0)
@@ -307,7 +309,9 @@ def tile_mla_pa_t_kernel(tc, h, w_cq, w_q, w_qr, out):
         quantise_h(1)
         quantise_weights(w2_codes, w2_scales, w2_grouped, 0)
         quantise_c(0)
-        regroup(nc.vector.tensor_copy, w2_grouped[:, 1], w2_raw[:, 1])
+        share = D_OUT // 2
+        regroup(nc.scalar.copy, w2_grouped[:, 1, :share], w2_raw[:, 1, :, :share])
+        regroup(nc.vector.tensor_copy, w2_grouped[:, 1, share:], w2_raw[:, 1, :, share:])
         transpose_h(2)
         compress(1)
         quantise_weights(w2_codes, w2_scales, w2_grouped, 1)
@@ -316,7 +320,6 @@ def tile_mla_pa_t_kernel(tc, h, w_cq, w_q, w_qr, out):
         rotate(0, 0)
         quantise_c(1)
         rotate(0, 1)
-        fill_rope_table(nc, table, size, fraction, quarter_turn, HALF, TILES)
         for n in range(3, len(steps) + 2):
             if n < len(steps):
                 transpose_h(n)

@@ -226,10 +226,10 @@ def tile_mla_pa_t_kernel(tc, h, w_cq, w_q, w_qr, out):
             )
             c_mx[n] = (codes, scales)
 
-        def store(b, first, count, heads=slice(0, N_H)):
+        def store(b, first, count, heads=slice(0, N_H), queue=nc.sync):
             rows = out[b].rearrange("n (p t) f -> p n t f", t=TILES)
             q_tile = out_tiles[(b, first // HALF)]
-            nc.sync.dma_start(
+            queue.dma_start(
                 out=rows[:, heads, first : first + count, :],
                 in_=q_tile[:, heads, first % HALF : first % HALF + count, :],
             )
@@ -240,9 +240,9 @@ def tile_mla_pa_t_kernel(tc, h, w_cq, w_q, w_qr, out):
             if first % HALF == 0:
                 out_tiles[(b, first // HALF)] = out_pool.tile([P, N_H, HALF, 2 * D_H], F32, name="q_tile")
             q_tile = out_tiles[(b, first // HALF)]
-            banks = []
-            for i in range(STEP):
-                for which, name in enumerate(("a_ps", "u_ps")):
+            banks = {}
+            for which, name in enumerate(("a_ps", "u_ps")):
+                for i in range(STEP):
                     product = psum.tile([P, D_OUT], F32, name=name)
                     nc.tensor.matmul_mx(
                         out=product[:],
@@ -253,13 +253,13 @@ def tile_mla_pa_t_kernel(tc, h, w_cq, w_q, w_qr, out):
                         start=True,
                         stop=True,
                     )
-                    banks.append(product)
+                    banks[(which, i)] = product
             for i in copy_order(n):
                 t = first + i
                 nc.scalar.copy(
-                    out=q_tile[:, :, t % HALF, 0:D_H], in_=banks[2 * i][:].rearrange("p (n f) -> p n f", n=N_H)
+                    out=q_tile[:, :, t % HALF, 0:D_H], in_=banks[(0, i)][:].rearrange("p (n f) -> p n f", n=N_H)
                 )
-                u_banks[(n, i)] = banks[2 * i + 1]
+                u_banks[(n, i)] = banks[(1, i)]
 
         def rotate(n, i):
             b, first = steps[n]
@@ -285,7 +285,7 @@ def tile_mla_pa_t_kernel(tc, h, w_cq, w_q, w_qr, out):
                     op=ADD,
                 )
                 if is_last:
-                    store(b, first + i, 1, slice(n0, n1))
+                    store(b, first + i, 1, slice(n0, n1), nc.scalar)
             if is_last:
                 return
             if n >= len(steps) - 2:

@@ -25,6 +25,8 @@ TILES = S // P
 PAIRS = D_H // 2
 HALF = 4
 STEP = 2
+SCALAR_BANKS = 5
+U_BANKS = 3
 STEADY = 3
 ROPE_BASE = 10000.0
 ROUND_MAGIC = 1.5 * 2.0**23
@@ -101,7 +103,7 @@ def tile_mla_pa_t_kernel(tc, h, w_cq, w_q, w_qr, out):
         x_pool = ctx.enter_context(tc.tile_pool(name="x", bufs=B * TILES // HALF))
         work = ctx.enter_context(tc.tile_pool(name="work", bufs=3))
         out_pool = ctx.enter_context(tc.tile_pool(name="outs", bufs=3))
-        psum = ctx.enter_context(tc.psum_pool(name="psum", bufs=STEP))
+        psum = ctx.enter_context(tc.psum_pool(name="psum", bufs=1))
 
         halves = [(b, half) for b in range(B) for half in range(TILES // HALF)]
         x_tiles = {}
@@ -174,7 +176,7 @@ def tile_mla_pa_t_kernel(tc, h, w_cq, w_q, w_qr, out):
             )
             banks = []
             for i in range(STEP):
-                xt = psum.tile([P, 2 * PASSES_1, P], F32, name="xt")
+                xt = psum.tile([P, 2 * PASSES_1, P], F32, name="scalar_bank", bufs=SCALAR_BANKS)
                 for g in range(PASSES_1):
                     word0 = ((first + i) % HALF) * (D_MODEL // 2) + g * 2 * P
                     for u in range(2):
@@ -200,7 +202,7 @@ def tile_mla_pa_t_kernel(tc, h, w_cq, w_q, w_qr, out):
             c_grouped[n] = work.tile([P, STEP, P, PACK], BF16, name="c_grouped", align_bytes=64)
             banks = []
             for i in range(STEP):
-                cq = psum.tile([P, PACK, P], F32, name="cq")
+                cq = psum.tile([P, PACK, P], F32, name="scalar_bank", bufs=SCALAR_BANKS)
                 for t in range(PACK):
                     for g in range(PASSES_1):
                         nc.tensor.matmul_mx(
@@ -241,9 +243,9 @@ def tile_mla_pa_t_kernel(tc, h, w_cq, w_q, w_qr, out):
                 out_tiles[(b, first // HALF)] = out_pool.tile([P, N_H, HALF, 2 * D_H], F32, name="q_tile")
             q_tile = out_tiles[(b, first // HALF)]
             banks = {}
-            for which, name in enumerate(("a_ps", "u_ps")):
+            for which, (name, bufs) in enumerate((("scalar_bank", SCALAR_BANKS), ("u_bank", U_BANKS))):
                 for i in range(STEP):
-                    product = psum.tile([P, D_OUT], F32, name=name)
+                    product = psum.tile([P, D_OUT], F32, name=name, bufs=bufs)
                     nc.tensor.matmul_mx(
                         out=product[:],
                         lhsT=codes_c[:, i, :].bitcast(FP8X4),

import math
from contextlib import ExitStack

import concourse.mybir as mybir
from concourse.masks import make_identity

F32 = mybir.dt.float32
BF16 = mybir.dt.bfloat16
I32 = mybir.dt.int32
U32 = mybir.dt.uint32
U8 = mybir.dt.uint8
FP8X4 = mybir.dt.float8_e4m3fn_x4
MULT = mybir.AluOpType.mult
ADD = mybir.AluOpType.add
SUBTRACT = mybir.AluOpType.subtract
SIN = mybir.ActivationFunctionType.Sin
ABS = mybir.ActivationFunctionType.Abs

P = 128
PACK = 4
B, S, D_MODEL, N_H, D_H, D_CQ = 4, 1024, 1024, 4, 128, 512
D_OUT = N_H * D_H
PASSES_1 = D_MODEL // (P * PACK)
TILES = S // P
PAIRS = D_H // 2
HALF = 4
STEP = 2
SCALAR_BANKS = 5
U_BANKS = 3
STEADY = 3
ROPE_BASE = 10000.0
ROUND_MAGIC = 1.5 * 2.0**23

FLOPS = 2 * B * S * (D_MODEL * D_CQ + D_CQ * 2 * D_OUT)


def rope_turns(nc, pool):
    position = pool.tile([P, TILES], F32)
    nc.gpsimd.iota(
        position[:],
        pattern=[[1, TILES]],
        base=0,
        channel_multiplier=TILES,
        allow_small_or_imprecise_dtypes=True,
    )
    ratio = ROPE_BASE ** (-1.0 / PAIRS)
    freq = pool.tile([P, PAIRS], F32)
    nc.vector.memset(freq[:, 0:1], 1.0)
    quarter_turn = pool.tile([P, 1], F32)
    nc.vector.tensor_scalar(
        out=quarter_turn[:], in0=freq[:, 0:1], scalar1=math.pi / 2.0, scalar2=0.0, op0=MULT, op1=ADD
    )
    for w in (1, 4, 16):
        for k in range(1, 4):
            nc.vector.tensor_scalar_mul(
                out=freq[:, k * w : (k + 1) * w], in0=freq[:, 0:w], scalar1=ratio ** (k * w)
            )

    shape = [P, TILES, PAIRS]
    turns = pool.tile(shape, F32)
    nc.vector.scalar_tensor_tensor(
        out=turns[:],
        in0=freq[:].unsqueeze(1).to_broadcast(shape),
        scalar=1.0 / (2.0 * math.pi),
        in1=position[:].unsqueeze(2).to_broadcast(shape),
        op0=MULT,
        op1=MULT,
    )
    return turns, quarter_turn


def turn_fractions(nc, pool, turns):
    shape = [P, TILES, PAIRS]
    whole = pool.tile(shape, F32)
    nc.vector.tensor_scalar(
        out=whole[:], in0=turns[:], scalar1=ROUND_MAGIC, scalar2=ROUND_MAGIC, op0=ADD, op1=SUBTRACT
    )
    fraction = pool.tile(shape, F32)
    nc.vector.tensor_sub(out=fraction[:], in0=turns[:], in1=whole[:])
    return fraction


def fill_rope_table(nc, table, size, fraction, quarter_turn):
    turn = 2.0 * math.pi
    nc.scalar.activation(out=table[:, :, 2, :], in_=fraction[:], func=SIN, scale=turn)
    nc.scalar.activation(out=size[:], in_=fraction[:], func=ABS)
    nc.scalar.activation(out=table[:, :, 0, :], in_=fraction[:], func=SIN, scale=-turn)
    nc.scalar.activation(out=table[:, :, 1, :], in_=size[:], func=SIN, scale=-turn, bias=quarter_turn[:])


def regroup(copy, grouped, raw):
    copy(
        out=grouped.rearrange("p (c i) t -> p c t i", i=4),
        in_=raw.rearrange("p t (c i) -> p c t i", i=4),
    )


def tile_mla_pa_t_kernel(tc, h, w_cq, w_q, w_qr, out):
    nc = tc.nc
    with ExitStack() as ctx:
        ctx.enter_context(tc.manual_schedule())
        consts = ctx.enter_context(tc.tile_pool(name="consts", bufs=1))
        x_pool = ctx.enter_context(tc.tile_pool(name="x", bufs=B * TILES // HALF))
        work = ctx.enter_context(tc.tile_pool(name="work", bufs=3))
        out_pool = ctx.enter_context(tc.tile_pool(name="outs", bufs=3))
        psum = ctx.enter_context(tc.psum_pool(name="psum", bufs=1))

        halves = [(b, half) for b in range(B) for half in range(TILES // HALF)]
        x_tiles = {}
        for b, half in halves:
            x_tiles[(b, half)] = x_pool.tile([P, HALF, D_MODEL], BF16, name="x")

        def load_h(b, half, first, count):
            rows = h[b].rearrange("(p t) k -> p t k", t=TILES)
            nc.sync.dma_start(
                out=x_tiles[(b, half)][:, first : first + count, :],
                in_=rows[:, half * HALF + first : half * HALF + first + count, :],
            )

        wc_raw = consts.tile([P, PASSES_1, PACK, D_CQ], BF16)
        w2_raw = consts.tile([P, 2, PACK, D_OUT], BF16)
        for g in range(PASSES_1):
            nc.sync.dma_start(
                out=wc_raw[:, g], in_=w_cq.rearrange("(g p j) c -> g p j c", g=PASSES_1, j=PACK)[g]
            )
        load_h(0, 0, 0, STEP)
        load_h(0, 0, STEP, STEP)
        nc.sync.dma_start(out=w2_raw[:, 0], in_=w_q.rearrange("(p j) n -> p j n", j=PACK))
        load_h(0, 1, 0, STEP)
        nc.sync.dma_start(out=w2_raw[:, 1], in_=w_qr.rearrange("(p j) n -> p j n", j=PACK))
        load_h(0, 1, STEP, STEP)
        for b, half in halves[2:]:
            load_h(b, half, 0, HALF)

        identity = consts.tile([P, P], F32)
        make_identity(nc, identity[:])
        turns, quarter_turn = rope_turns(nc, consts)

        wc_grouped = consts.tile([P, PASSES_1, D_CQ, PACK], BF16, align_bytes=64)
        wc_codes = consts.tile([P, PASSES_1, D_CQ], U32, align_bytes=64)
        wc_scales = consts.tile([P, PASSES_1, D_CQ], U8, align_bytes=64)
        w2_grouped = consts.tile([P, 2, D_OUT, PACK], BF16, align_bytes=64)
        w2_codes = consts.tile([P, 2, D_OUT], U32, align_bytes=64)
        w2_scales = consts.tile([P, 2, D_OUT], U8, align_bytes=64)

        def regroup_first_weights(g):
            nc.vector.tensor_copy(
                out=wc_grouped[:, g].rearrange("p (t m) j -> p m t j", t=PACK),
                in_=wc_raw[:, g].rearrange("p j (m t) -> p m t j", t=PACK),
            )

        def quantise_weights(codes, scales, grouped, g):
            nc.vector.quantize_mx(
                out=codes[:, g].bitcast(FP8X4),
                scales=scales[:, g],
                in_=grouped[:, g].rearrange("p c j -> p (c j)"),
            )

        steps = [(b, first) for b in range(B) for first in range(0, TILES, STEP)]
        h_grouped = {}
        h_mx = {}
        c_grouped = {}
        c_mx = {}
        out_tiles = {}
        u_banks = {}

        def copy_order(n):
            return range(STEP) if n < STEADY else range(STEP - 1, -1, -1)

        def transpose_h(n):
            b, first = steps[n]
            x_words = x_tiles[(b, first // HALF)][:].rearrange("p t k -> p (t k)").bitcast(F32)
            h_grouped[n] = work.tile([P, STEP * PASSES_1 * P * PACK], BF16, name="h_grouped", align_bytes=64)
            grouped_words = h_grouped[n][:].bitcast(F32).rearrange(
                "p (i g r u) -> p i g r u", i=STEP, g=PASSES_1, u=2
            )
            banks = []
            for i in range(STEP):
                xt = psum.tile([P, 2 * PASSES_1, P], F32, name="scalar_bank", bufs=SCALAR_BANKS)
                for g in range(PASSES_1):
                    word0 = ((first + i) % HALF) * (D_MODEL // 2) + g * 2 * P
                    for u in range(2):
                        nc.tensor.transpose(
                            xt[:, 2 * g + u, :], x_words[:, word0 + u : word0 + 2 * P : 2], identity[:]
                        )
                banks.append(xt)
            for i in copy_order(n):
                nc.scalar.copy(out=grouped_words[:, i], in_=banks[i][:].rearrange("p (g u) r -> p g r u", u=2))

        def quantise_h(n):
            codes = work.tile([P, STEP, PASSES_1, P], U32, name="h_codes", align_bytes=64)
            scales = work.tile([P, STEP, PASSES_1, P], U8, name="h_scales", align_bytes=64)
            nc.vector.quantize_mx(
                out=codes[:].rearrange("p i g r -> p (i g r)").bitcast(FP8X4),
                scales=scales[:].rearrange("p i g r -> p (i g r)"),
                in_=h_grouped[n][:],
            )
            h_mx[n] = (codes, scales)

        def compress(n):
            codes_h, scales_h = h_mx[n]
            c_grouped[n] = work.tile([P, STEP, P, PACK], BF16, name="c_grouped", align_bytes=64)
            banks = []
            for i in range(STEP):
                cq = psum.tile([P, PACK, P], F32, name="scalar_bank", bufs=SCALAR_BANKS)
                for t in range(PACK):
                    for g in range(PASSES_1):
                        nc.tensor.matmul_mx(
                            out=cq[:, t, :],
                            lhsT=wc_codes[:, g, t * P : (t + 1) * P].bitcast(FP8X4),
                            lhsT_scale=wc_scales[:, g, t * P : (t + 1) * P],
                            rhs=codes_h[:, i, g, :].bitcast(FP8X4),
                            rhs_scale=scales_h[:, i, g, :],
                            start=(g == 0),
                            stop=(g == PASSES_1 - 1),
                        )
                banks.append(cq)
            for i in copy_order(n):
                nc.scalar.copy(out=c_grouped[n][:, i], in_=banks[i][:].rearrange("p t r -> p r t"))

        def quantise_c(n):
            codes = work.tile([P, STEP, P], U32, name="c_codes", align_bytes=64)
            scales = work.tile([P, STEP, P], U8, name="c_scales", align_bytes=64)
            nc.vector.quantize_mx(
                out=codes[:].rearrange("p i r -> p (i r)").bitcast(FP8X4),
                scales=scales[:].rearrange("p i r -> p (i r)"),
                in_=c_grouped[n][:].rearrange("p i r t -> p (i r t)"),
            )
            c_mx[n] = (codes, scales)

        def store(b, first, count, heads=slice(0, N_H), queue=nc.sync):
            rows = out[b].rearrange("n (p t) f -> p n t f", t=TILES)
            q_tile = out_tiles[(b, first // HALF)]
            queue.dma_start(
                out=rows[:, heads, first : first + count, :],
                in_=q_tile[:, heads, first % HALF : first % HALF + count, :],
            )

        def project(n):
            b, first = steps[n]
            codes_c, scales_c = c_mx[n]
            if first % HALF == 0:
                out_tiles[(b, first // HALF)] = out_pool.tile([P, N_H, HALF, 2 * D_H], F32, name="q_tile")
            q_tile = out_tiles[(b, first // HALF)]
            banks = {}
            for which, (name, bufs) in enumerate((("scalar_bank", SCALAR_BANKS), ("u_bank", U_BANKS))):
                for i in range(STEP):
                    product = psum.tile([P, D_OUT], F32, name=name, bufs=bufs)
                    nc.tensor.matmul_mx(
                        out=product[:],
                        lhsT=codes_c[:, i, :].bitcast(FP8X4),
                        lhsT_scale=scales_c[:, i, :],
                        rhs=w2_codes[:, which, :].bitcast(FP8X4),
                        rhs_scale=w2_scales[:, which, :],
                        start=True,
                        stop=True,
                    )
                    banks[(which, i)] = product
            for i in copy_order(n):
                t = first + i
                nc.scalar.copy(
                    out=q_tile[:, :, t % HALF, 0:D_H], in_=banks[(0, i)][:].rearrange("p (n f) -> p n f", n=N_H)
                )
                u_banks[(n, i)] = banks[(1, i)]

        def rotate(n, i):
            b, first = steps[n]
            q_tile = out_tiles[(b, first // HALF)]
            is_last = n == len(steps) - 1 and i == STEP - 1
            products = work.tile([P, 2, N_H, PAIRS, 2], F32, name="products")
            u_pairs = u_banks[(n, i)][:].rearrange("p (n i x) -> p n i x", n=N_H, x=2)
            for n0, n1 in ((0, 2), (2, N_H)) if is_last else ((0, N_H),):
                shape = [P, n1 - n0, PAIRS, 2]
                for x in range(2):
                    factors = table[:, first + i, 1 - x : 3 - x, :].rearrange("p e i -> p i e")
                    nc.vector.tensor_tensor(
                        out=products[:, x, n0:n1],
                        in0=u_pairs[:, n0:n1, :, x].unsqueeze(3).to_broadcast(shape),
                        in1=factors.unsqueeze(1).to_broadcast(shape),
                        op=MULT,
                    )
                add = nc.vector.tensor_tensor if is_last else nc.gpsimd.tensor_tensor
                add(
                    out=q_tile[:, n0:n1, (first + i) % HALF, D_H : 2 * D_H],
                    in0=products[:, 0, n0:n1].rearrange("p n i e -> p n (i e)"),
                    in1=products[:, 1, n0:n1].rearrange("p n i e -> p n (i e)"),
                    op=ADD,
                )
                if is_last:
                    store(b, first + i, 1, slice(n0, n1), nc.scalar)
            if is_last:
                return
            if n >= len(steps) - 2:
                store(b, first + i, 1)
            elif i == STEP - 1:
                store(b, first, STEP)

        fraction = turn_fractions(nc, consts, turns)
        table = consts.tile([P, TILES, 3, PAIRS], F32)
        size = consts.tile([P, TILES, PAIRS], F32)
        fill_rope_table(nc, table, size, fraction, quarter_turn)
        regroup_first_weights(0)
        regroup_first_weights(1)
        quantise_weights(wc_codes, wc_scales, wc_grouped, 0)
        quantise_weights(wc_codes, wc_scales, wc_grouped, 1)
        transpose_h(0)
        quantise_h(0)
        transpose_h(1)
        compress(0)
        regroup(nc.vector.tensor_copy, w2_grouped[:, 0], w2_raw[:, 0])
        quantise_h(1)
        quantise_weights(w2_codes, w2_scales, w2_grouped, 0)
        quantise_c(0)
        share = D_OUT // 2
        regroup(nc.scalar.copy, w2_grouped[:, 1, :share], w2_raw[:, 1, :, :share])
        regroup(nc.vector.tensor_copy, w2_grouped[:, 1, share:], w2_raw[:, 1, :, share:])
        transpose_h(2)
        compress(1)
        quantise_weights(w2_codes, w2_scales, w2_grouped, 1)
        project(0)
        quantise_h(2)
        rotate(0, 0)
        quantise_c(1)
        rotate(0, 1)
        for n in range(3, len(steps) + 2):
            if n < len(steps):
                transpose_h(n)
                quantise_h(n)
            if n <= len(steps):
                compress(n - 1)
            project(n - 2)
            rotate(n - 2, 0)
            if n <= len(steps):
                quantise_c(n - 1)
            rotate(n - 2, 1)
